import numpy as np
import ml_dtypes


def mxq(x, axis, fmt="e4m3"):
    dtype, down = {"e4m3": (ml_dtypes.float8_e4m3fn, 7), "e5m2": (ml_dtypes.float8_e5m2, 14)}[fmt]
    v = np.moveaxis(np.asarray(x, np.float32).astype(ml_dtypes.bfloat16).astype(np.float64), axis, -1)
    blocks = v.reshape(v.shape[:-1] + (-1, 32))
    amax = np.abs(blocks).max(-1, keepdims=True)
    byte = np.maximum(np.where(amax > 0, np.frexp(amax)[1] - 1 + 127, 0) - down, 1)
    scale = np.exp2(byte - 127.0)
    codes = (blocks / scale).astype(np.float32).astype(dtype).astype(np.float64)
    return np.moveaxis((codes * scale).reshape(v.shape), -1, axis)


WIDE = False


def mx_kscale(k):
    if not WIDE:
        return np.ones(k)
    levels = np.array([10, -10, 5, -5, 0])
    a = np.random.permutation(np.resize(levels, k // 512 * 4)).reshape(k // 512, 4)
    idx = np.arange(k)
    return np.exp2(a[idx // 512, idx % 128 // 32])


BF16 = ml_dtypes.bfloat16


def bf(x):
    return np.asarray(x, np.float32).astype(BF16)


def f64(x):
    return np.asarray(x).astype(np.float64)


E2M1 = np.array([0.0, 0.5, 1.0, 1.5, 2.0, 3.0, 4.0, 6.0, -0.0, -0.5, -1.0, -1.5, -2.0, -3.0, -4.0, -6.0])


def pack_weight(w, fmt):
    k, n = w.shape
    w = f64(bf(w)).reshape(k // 32, 32, n)
    amax = np.abs(w).max(1)
    if fmt == "e4m3":
        byte = np.frexp(amax)[1] - 1 + 127 - 7
    else:
        mant, ex = np.frexp(amax / 6.0)
        byte = np.where(mant > 0.5, ex, ex - 1) + 127
    byte = np.clip(np.where(amax > 0, byte, 1), 1, 254)
    scaled = (w * np.exp2(127.0 - byte)[:, None, :]).reshape(k, n).astype(np.float32)
    by_word = np.ascontiguousarray(scaled.reshape(k // 512, 128, 4, n).transpose(0, 1, 3, 2))
    if fmt == "e4m3":
        words = by_word.astype(ml_dtypes.float8_e4m3fn).view(np.uint8)
    else:
        c = by_word.astype(ml_dtypes.float4_e2m1fn).view(np.uint8) & 0xF
        words = c[..., 0::2] | (c[..., 1::2] << 4)
    return np.ascontiguousarray(words), np.ascontiguousarray(byte.astype(np.uint8).reshape(k // 512, 16, n))


def unpack_weight(words, scales, fmt):
    g, p, n, _ = words.shape
    if fmt == "e4m3":
        vals = np.ascontiguousarray(words).view(ml_dtypes.float8_e4m3fn).astype(np.float64)
    else:
        nib = np.empty((g, p, n, 4), np.uint8)
        nib[..., 0::2] = words & 0xF
        nib[..., 1::2] = words >> 4
        vals = E2M1[nib]
    vals = vals * np.repeat(np.exp2(scales.astype(np.float64) - 127.0), 8, axis=1)[..., None]
    return vals.transpose(0, 1, 3, 2).reshape(g * 512, n)


B, T, D, O = 8, 32, 4096, 4096


def erf(z):
    a = np.clip(z, -6.0, 6.0)
    q = 2.0 * a * a
    term = a.copy()
    total = a.copy()
    for k in range(1, 130):
        term = term * q / (2 * k + 1)
        total = total + term
    return 2.0 / np.sqrt(np.pi) * np.exp(-a * a) * total


def gelu_exact(v):
    return 0.5 * v * (1.0 + erf(v / np.sqrt(2.0)))


def setup_inputs():
    s = mx_kscale(D)
    x = np.random.standard_normal((B, T, D)) * s
    lengths = np.random.randint(T // 4, T + 1, size=B)
    lengths[np.random.randint(B)] = T
    pad = np.arange(T)[None, :] >= lengths[:, None]
    x = np.where(pad[:, :, None], -1.0, x)
    w = np.random.standard_normal((O, D)) / np.sqrt(D) / s[None, :]
    words, scales = pack_weight(np.ascontiguousarray(w.T), "e4m3")
    return {"x": bf(x), "W_words": words, "W_scales": scales, "b": bf(np.random.standard_normal(O) * 0.3)}


def reference(x, W_words, W_scales, b):
    x = f64(x)
    valid = ~np.all(x == -1.0, axis=-1)
    y = gelu_exact((mxq(x, 2, "e4m3") @ unpack_weight(W_words, W_scales, "e4m3")) + f64(b))
    vf = valid[..., None].astype(np.float64)
    n = np.sum(vf, axis=1)
    mean = np.sum(y * vf, axis=1) / n
    diff = (y - mean[:, None, :]) * vf
    var = np.sum(diff * diff, axis=1) / np.maximum(n - 1.0, 1.0)
    std = np.where(n > 1.0, np.sqrt(var), np.zeros_like(var))
    out = np.concatenate([std, mean], axis=-1)
    return np.where(np.isnan(out), np.zeros_like(out), out)

@@ -1,0 +1,291 @@
+from contextlib import ExitStack
+
+import concourse.mybir as mybir
+from concourse.masks import make_identity
+
+F32 = mybir.dt.float32
+BF16 = mybir.dt.bfloat16
+I32 = mybir.dt.int32
+U32 = mybir.dt.uint32
+U8 = mybir.dt.uint8
+FP8X4 = mybir.dt.float8_e4m3fn_x4
+ALU = mybir.AluOpType
+ACT = mybir.ActivationFunctionType
+AX = mybir.AxisListType
+
+P = 128
+SAMPLES = 8
+T = 32
+TOKENS = SAMPLES * T
+K_DIM = 4096
+N_DIM = 4096
+K_PASS = 4 * P
+GROUPS = K_DIM // K_PASS
+N_TILES = N_DIM // P
+BANKS = 8
+HALF_K = K_DIM // 2
+
+PIECE_OPERANDS = 16
+ROUND_TILES = (8, 8, 8, 4, 4)
+BLOCK_TILES = 8
+BLOCKS = N_TILES // BLOCK_TILES
+
+FLOPS = 2 * TOKENS * K_DIM * N_DIM
+
+
+def tile_linearnnencoder_w_kernel(tc, x, W_words, W_scales, b, out):
+    nc = tc.nc
+    with ExitStack() as ctx:
+        ctx.enter_context(tc.manual_schedule())
+        keep = ctx.enter_context(tc.tile_pool(name="keep", bufs=1))
+        small = ctx.enter_context(tc.tile_pool(name="small", bufs=2))
+        values = ctx.enter_context(tc.tile_pool(name="values", bufs=2 * BANKS))
+        psum = ctx.enter_context(tc.psum_pool(name="psum", bufs=1))
+
+        b_rows = keep.tile([P, P], BF16)
+        nc.gpsimd.memset(b_rows[:], 0.0)
+        ident = keep.tile([P, P], F32)
+        make_identity(nc, ident[:])
+        w_planes = keep.tile([P, GROUPS // 4, N_DIM], U8, align_bytes=64)
+        nc.vector.memset(w_planes[:].bitcast(I32), 0)
+
+        x_rows = x.rearrange("b t k -> (b t) k")
+        x_sb = {}
+        for h in range(2):
+            for i in range(2):
+                x_piece = keep.tile([P, HALF_K], BF16, name="x_%d_%d" % (i, h))
+                nc.sync.dma_start(
+                    out=x_piece[:], in_=x_rows[i * P : (i + 1) * P, h * HALF_K : (h + 1) * HALF_K]
+                )
+                x_sb[(i, h)] = x_piece
+        nc.sync.dma_start(out=b_rows[0:N_TILES, :], in_=b.rearrange("(j o) -> j o", o=P))
+        half_n = N_DIM // 2
+        for nh in range(2):
+            n_half = slice(nh * half_n, (nh + 1) * half_n)
+            for c in range(GROUPS // 4):
+                for quadrant in range(4):
+                    nc.sync.dma_start(
+                        out=w_planes[32 * quadrant : 32 * quadrant + 16, c, n_half].bitcast(I32),
+                        in_=W_scales[
+                            4 * c : 4 * c + 4, 4 * quadrant : 4 * quadrant + 4, n_half
+                        ].bitcast(I32),
+                    )
+        w_view = W_words.rearrange("g p n t -> g p (n t)").bitcast(I32)
+        w_pieces = {}
+        first_tile = 0
+        for r, tiles in enumerate(ROUND_TILES):
+            groups = PIECE_OPERANDS // tiles
+            n_cols = slice(first_tile * P, (first_tile + tiles) * P)
+            for f in range(GROUPS // groups):
+                w_piece = keep.tile(
+                    [P, groups, tiles * P], U32, name="w_%d_%d" % (r, f), align_bytes=64
+                )
+                nc.sync.dma_start(
+                    out=w_piece[:].bitcast(I32),
+                    in_=w_view[f * groups : (f + 1) * groups, :, n_cols].rearrange("g p n -> p g n"),
+                )
+                w_pieces[(r, f)] = w_piece
+            first_tile += tiles
+
+        junk = keep.tile([P, HALF_K], BF16)
+        distance = {}
+        for i in range(2):
+            distance[i] = keep.tile([P, 2], F32, name="distance%d" % i)
+        for h in range(2):
+            for i in range(2):
+                nc.scalar.activation(
+                    out=junk[:],
+                    in_=x_sb[(i, h)][:],
+                    func=ACT.Abs,
+                    bias=1.0,
+                    scale=1.0,
+                    accum_out=distance[i][:, h : h + 1],
+                )
+
+        x_t = {}
+        for g in range(GROUPS):
+            x_t[g] = psum.tile([P, 2, TOKENS], F32, tag="bank%d" % g, name="x_t%d" % g)
+            first_word = (K_PASS // 2) * (g % 4)
+            for i in range(2):
+                words = x_sb[(i, g // 4)][:].bitcast(F32)
+                for u in range(2):
+                    nc.tensor.transpose(
+                        x_t[g][:, u, i * P : (i + 1) * P],
+                        words[:, first_word + u : first_word + K_PASS // 2 : 2],
+                        ident[:],
+                    )
+        grouped = keep.tile([P, GROUPS, 4 * TOKENS], BF16, align_bytes=64)
+        x_codes = keep.tile([P, GROUPS, TOKENS], U32, align_bytes=64)
+        x_planes = keep.tile([P, GROUPS, TOKENS], U8, align_bytes=64)
+
+        def quantise(g):
+            nc.vector.quantize_mx(
+                out=x_codes[:, g, :].bitcast(FP8X4), scales=x_planes[:, g, :], in_=grouped[:, g, :]
+            )
+
+        for g in range(GROUPS):
+            nc.vector.tensor_copy(
+                out=grouped[:, g, :].bitcast(F32).rearrange("p (k u) -> p k u", u=2),
+                in_=x_t[g][:].rearrange("p u k -> p k u"),
+            )
+            if g > 0:
+                quantise(g - 1)
+        quantise(GROUPS - 1)
+
+        b_f32 = keep.tile([P, P], F32)
+        nc.vector.tensor_copy(out=b_f32[:], in_=b_rows[:])
+        b_t = psum.tile([P, P], F32, tag="bank6")
+        nc.tensor.transpose(b_t[:], b_f32[:], ident[:])
+        bias = keep.tile([P, N_TILES], F32)
+        nc.vector.tensor_copy(out=bias[:], in_=b_t[:, 0:N_TILES])
+        shift = keep.tile([P, N_TILES], F32)
+        nc.scalar.activation(out=shift[:], in_=bias[:], func=ACT.Gelu)
+
+        mask_ps = psum.tile([P, TOKENS], F32, tag="bank7")
+        for i in range(2):
+            valid = keep.tile([P, 1], F32, name="valid%d" % i)
+            nc.vector.tensor_scalar(
+                out=valid[:],
+                in0=distance[i][:, 0:1],
+                scalar1=distance[i][:, 1:2],
+                scalar2=0.0,
+                op0=ALU.add,
+                op1=ALU.is_gt,
+            )
+            nc.tensor.matmul(
+                out=mask_ps[:, i * P : (i + 1) * P],
+                lhsT=valid[:, 0:1].to_broadcast([P, P]),
+                rhs=ident[:],
+                start=True,
+                stop=True,
+            )
+        mask = keep.tile([P, TOKENS], F32)
+        nc.vector.tensor_copy(out=mask[:], in_=mask_ps[:])
+        count = keep.tile([P, SAMPLES], F32)
+        nc.vector.tensor_reduce(
+            out=count[:], in_=mask[:].rearrange("p (b t) -> p b t", t=T), axis=AX.X, op=ALU.add
+        )
+        inv_n = keep.tile([P, SAMPLES], F32)
+        nc.vector.tensor_scalar(out=inv_n[:], in0=count[:], scalar1=1.0, scalar2=None, op0=ALU.max)
+        nc.vector.reciprocal(out=inv_n[:], in_=inv_n[:])
+        inv_n1 = keep.tile([P, SAMPLES], F32)
+        nc.vector.tensor_scalar(
+            out=inv_n1[:], in0=count[:], scalar1=-1.0, scalar2=1.0, op0=ALU.add, op1=ALU.max
+        )
+        nc.vector.reciprocal(out=inv_n1[:], in_=inv_n1[:])
+        nc.vector.scalar_tensor_tensor(
+            out=inv_n1[:], in0=count[:], scalar=1.0, in1=inv_n1[:], op0=ALU.is_gt, op1=ALU.mult
+        )
+        some = keep.tile([P, SAMPLES], F32)
+        nc.vector.tensor_scalar(out=some[:], in0=count[:], scalar1=1.0, scalar2=None, op0=ALU.min)
+        shift_b = keep.tile([P, SAMPLES, N_TILES], F32)
+        nc.vector.tensor_tensor(
+            out=shift_b[:],
+            in0=shift[:].unsqueeze(1).to_broadcast([P, SAMPLES, N_TILES]),
+            in1=some[:].unsqueeze(2).to_broadcast([P, SAMPLES, N_TILES]),
+            op=ALU.mult,
+        )
+
+        sums = keep.tile([P, 2, SAMPLES, N_TILES], F32)
+        results = {}
+        for block in range(BLOCKS):
+            results[block] = keep.tile([P, P], F32, name="results%d" % block)
+        out_blocks = out.rearrange(
+            "b (s r j o) -> r b s j o", s=2, r=BLOCKS, j=BLOCK_TILES, o=P
+        )
+
+        res_t = {}
+
+        def root_and_transpose(block):
+            std = results[block][:].rearrange("p (b s j) -> p b s j", b=SAMPLES, s=2)[:, :, 0, :]
+            nc.scalar.activation(out=std, in_=std, func=ACT.Sqrt)
+            res_t[block] = psum.tile([P, P], F32, tag="bank%d" % block, name="res_t%d" % block)
+            nc.tensor.transpose(res_t[block][:], results[block][:], ident[:])
+
+        first_tile = 0
+        for r, tiles in enumerate(ROUND_TILES):
+            groups = PIECE_OPERANDS // tiles
+            acc = {}
+            for jl in range(tiles):
+                j = first_tile + jl
+                acc[jl] = psum.tile([P, TOKENS], F32, tag="bank%d" % (j % BANKS), name="acc%d" % j)
+            for f in range(GROUPS // groups):
+                for jl in range(tiles):
+                    j = first_tile + jl
+                    for gl in range(groups):
+                        g = f * groups + gl
+                        nc.tensor.matmul_mx(
+                            out=acc[jl][:],
+                            lhsT=w_pieces[(r, f)][:, gl, jl * P : (jl + 1) * P].bitcast(FP8X4),
+                            lhsT_scale=w_planes[4 * (g % 4) : P, g // 4, j * P : (j + 1) * P],
+                            rhs=x_codes[:, g, :].bitcast(FP8X4),
+                            rhs_scale=x_planes[:, g, :],
+                            start=(g == 0),
+                            stop=(g == GROUPS - 1),
+                        )
+            z = {}
+            for jl in range(tiles):
+                j = first_tile + jl
+                z[jl] = values.tile([P, 2, TOKENS], F32, tag="z", name="z%d" % j)
+                nc.scalar.activation(
+                    out=z[jl][:, 0, :], in_=acc[jl][:], func=ACT.Gelu, bias=bias[:, j : j + 1], scale=1.0
+                )
+                nc.vector.scalar_tensor_tensor(
+                    out=z[jl][:, 0, :],
+                    in0=z[jl][:, 0, :],
+                    scalar=shift[:, j : j + 1],
+                    in1=mask[:],
+                    op0=ALU.subtract,
+                    op1=ALU.mult,
+                )
+            for jl in range(tiles):
+                j = first_tile + jl
+                nc.scalar.activation(out=z[jl][:, 1, :], in_=z[jl][:, 0, :], func=ACT.Square)
+                nc.vector.tensor_reduce(
+                    out=sums[:, :, :, j],
+                    in_=z[jl][:].rearrange("p s (b t) -> p s b t", t=T),
+                    axis=AX.X,
+                    op=ALU.add,
+                )
+            if r == len(ROUND_TILES) - 1:
+                for block in range(BLOCKS - 1):
+                    root_and_transpose(block)
+            tile_cols = slice(first_tile, first_tile + tiles)
+            shape = [P, SAMPLES, tiles]
+            block = first_tile // BLOCK_TILES
+            in_block = slice(first_tile % BLOCK_TILES, first_tile % BLOCK_TILES + tiles)
+            res = results[block][:].rearrange("p (b s j) -> p b s j", b=SAMPLES, s=2)
+            mean_z = small.tile(shape, F32, tag="mean_z", name="mean_z%d" % r)
+            nc.vector.tensor_tensor(
+                out=mean_z[:],
+                in0=sums[:, 0, :, tile_cols],
+                in1=inv_n[:].unsqueeze(2).to_broadcast(shape),
+                op=ALU.mult,
+            )
+            nc.vector.tensor_tensor(
+                out=res[:, :, 1, in_block], in0=mean_z[:], in1=shift_b[:, :, tile_cols], op=ALU.add
+            )
+            spread = small.tile(shape, F32, tag="spread", name="spread%d" % r)
+            nc.vector.tensor_tensor(
+                out=spread[:], in0=sums[:, 0, :, tile_cols], in1=mean_z[:], op=ALU.mult
+            )
+            nc.vector.tensor_tensor(
+                out=spread[:], in0=sums[:, 1, :, tile_cols], in1=spread[:], op=ALU.subtract
+            )
+            nc.vector.scalar_tensor_tensor(
+                out=res[:, :, 0, in_block],
+                in0=spread[:],
+                scalar=0.0,
+                in1=inv_n1[:].unsqueeze(2).to_broadcast(shape),
+                op0=ALU.max,
+                op1=ALU.mult,
+            )
+            first_tile += tiles
+        root_and_transpose(BLOCKS - 1)
+        for block in range(BLOCKS):
+            res_sb = keep.tile([P, P], F32, name="res_sb%d" % block)
+            if block % 2 == 0:
+                nc.scalar.copy(out=res_sb[:], in_=res_t[block][:])
+            else:
+                nc.vector.tensor_copy(out=res_sb[:], in_=res_t[block][:])
+            nc.sync.dma_start(out=out_blocks[block], in_=res_sb[:])

@@ -17,6 +17,7 @@ P = 128
 SAMPLES = 8
 T = 32
 TOKENS = SAMPLES * T
+TOKEN_TILES = TOKENS // P
 K_DIM = 4096
 N_DIM = 4096
 K_PASS = 4 * P
@@ -24,6 +25,9 @@ GROUPS = K_DIM // K_PASS
 N_TILES = N_DIM // P
 BANKS = 8
 HALF_K = K_DIM // 2
+HALF_N = N_DIM // 2
+
+PAD_WORD = -(1.0 + 0xBF80 / 2.0**23)
 
 PIECE_OPERANDS = 16
 ROUND_TILES = (8, 8, 8, 4, 4)
@@ -46,34 +50,36 @@ def tile_linearnnencoder_w_kernel(tc, x, W_words, W_scales, b, out):
         nc.gpsimd.memset(b_rows[:], 0.0)
         ident = keep.tile([P, P], F32)
         make_identity(nc, ident[:])
+        warm = keep.tile([P, 1], F32)
+        nc.vector.memset(warm[:], 0.0)
+        nc.scalar.dma_start(out=b_rows[0:N_TILES, :], in_=b.rearrange("(j o) -> j o", o=P))
+        nc.scalar.activation(out=warm[:], in_=warm[:], func=ACT.Gelu)
         w_planes = keep.tile([P, GROUPS // 4, N_DIM], U8, align_bytes=64)
         nc.vector.memset(w_planes[:].bitcast(I32), 0)
 
         x_rows = x.rearrange("b t k -> (b t) k")
         x_sb = {}
-        for h in range(2):
-            for i in range(2):
+        for i in range(TOKEN_TILES):
+            for h in range(2):
                 x_piece = keep.tile([P, HALF_K], BF16, name="x_%d_%d" % (i, h))
                 nc.sync.dma_start(
                     out=x_piece[:], in_=x_rows[i * P : (i + 1) * P, h * HALF_K : (h + 1) * HALF_K]
                 )
                 x_sb[(i, h)] = x_piece
-        nc.sync.dma_start(out=b_rows[0:N_TILES, :], in_=b.rearrange("(j o) -> j o", o=P))
-        half_n = N_DIM // 2
-        for nh in range(2):
-            n_half = slice(nh * half_n, (nh + 1) * half_n)
-            for c in range(GROUPS // 4):
-                for quadrant in range(4):
-                    nc.sync.dma_start(
-                        out=w_planes[32 * quadrant : 32 * quadrant + 16, c, n_half].bitcast(I32),
-                        in_=W_scales[
-                            4 * c : 4 * c + 4, 4 * quadrant : 4 * quadrant + 4, n_half
-                        ].bitcast(I32),
-                    )
         w_view = W_words.rearrange("g p n t -> g p (n t)").bitcast(I32)
         w_pieces = {}
         first_tile = 0
         for r, tiles in enumerate(ROUND_TILES):
+            if (first_tile * P) % HALF_N == 0:
+                n_half = slice(first_tile * P, first_tile * P + HALF_N)
+                for c in range(GROUPS // 4):
+                    for quadrant in range(4):
+                        nc.sync.dma_start(
+                            out=w_planes[32 * quadrant : 32 * quadrant + 16, c, n_half].bitcast(I32),
+                            in_=W_scales[
+                                4 * c : 4 * c + 4, 4 * quadrant : 4 * quadrant + 4, n_half
+                            ].bitcast(I32),
+                        )
             groups = PIECE_OPERANDS // tiles
             n_cols = slice(first_tile * P, (first_tile + tiles) * P)
             for f in range(GROUPS // groups):
@@ -87,83 +93,87 @@ def tile_linearnnencoder_w_kernel(tc, x, W_words, W_scales, b, out):
                 w_pieces[(r, f)] = w_piece
             first_tile += tiles
 
-        junk = keep.tile([P, HALF_K], BF16)
-        distance = {}
-        for i in range(2):
-            distance[i] = keep.tile([P, 2], F32, name="distance%d" % i)
-        for h in range(2):
-            for i in range(2):
-                nc.scalar.activation(
-                    out=junk[:],
-                    in_=x_sb[(i, h)][:],
-                    func=ACT.Abs,
-                    bias=1.0,
-                    scale=1.0,
-                    accum_out=distance[i][:, h : h + 1],
-                )
-
-        x_t = {}
-        for g in range(GROUPS):
-            x_t[g] = psum.tile([P, 2, TOKENS], F32, tag="bank%d" % g, name="x_t%d" % g)
-            first_word = (K_PASS // 2) * (g % 4)
-            for i in range(2):
-                words = x_sb[(i, g // 4)][:].bitcast(F32)
-                for u in range(2):
-                    nc.tensor.transpose(
-                        x_t[g][:, u, i * P : (i + 1) * P],
-                        words[:, first_word + u : first_word + K_PASS // 2 : 2],
-                        ident[:],
-                    )
-        grouped = keep.tile([P, GROUPS, 4 * TOKENS], BF16, align_bytes=64)
-        x_codes = keep.tile([P, GROUPS, TOKENS], U32, align_bytes=64)
-        x_planes = keep.tile([P, GROUPS, TOKENS], U8, align_bytes=64)
-
-        def quantise(g):
-            nc.vector.quantize_mx(
-                out=x_codes[:, g, :].bitcast(FP8X4), scales=x_planes[:, g, :], in_=grouped[:, g, :]
-            )
-
-        for g in range(GROUPS):
-            nc.vector.tensor_copy(
-                out=grouped[:, g, :].bitcast(F32).rearrange("p (k u) -> p k u", u=2),
-                in_=x_t[g][:].rearrange("p u k -> p k u"),
-            )
-            if g > 0:
-                quantise(g - 1)
-        quantise(GROUPS - 1)
-
         b_f32 = keep.tile([P, P], F32)
         nc.vector.tensor_copy(out=b_f32[:], in_=b_rows[:])
-        b_t = psum.tile([P, P], F32, tag="bank6")
+        b_t = psum.tile([P, P], F32, tag="bank7")
         nc.tensor.transpose(b_t[:], b_f32[:], ident[:])
         bias = keep.tile([P, N_TILES], F32)
         nc.vector.tensor_copy(out=bias[:], in_=b_t[:, 0:N_TILES])
-        shift = keep.tile([P, N_TILES], F32)
-        nc.scalar.activation(out=shift[:], in_=bias[:], func=ACT.Gelu)
 
-        mask_ps = psum.tile([P, TOKENS], F32, tag="bank7")
-        for i in range(2):
-            valid = keep.tile([P, 1], F32, name="valid%d" % i)
+        junk = keep.tile([P, HALF_K // 2], F32)
+        valid = {}
+        ident_valid = {}
+        for i in range(TOKEN_TILES):
+            distance = keep.tile([P, 2], F32, name="distance%d" % i)
+            for h in range(2):
+                nc.scalar.activation(
+                    out=junk[:],
+                    in_=x_sb[(i, h)][:].bitcast(F32),
+                    func=ACT.Abs,
+                    bias=-PAD_WORD,
+                    scale=1.0,
+                    accum_out=distance[:, h : h + 1],
+                )
+            valid[i] = keep.tile([P, 1], F32, name="valid%d" % i)
             nc.vector.tensor_scalar(
-                out=valid[:],
-                in0=distance[i][:, 0:1],
-                scalar1=distance[i][:, 1:2],
+                out=valid[i][:],
+                in0=distance[:, 0:1],
+                scalar1=distance[:, 1:2],
                 scalar2=0.0,
                 op0=ALU.add,
                 op1=ALU.is_gt,
             )
+            ident_valid[i] = keep.tile([P, P], F32, name="ident_valid%d" % i)
+            nc.vector.tensor_scalar(
+                out=ident_valid[i][:], in0=ident[:], scalar1=valid[i][:, 0:1], scalar2=None, op0=ALU.mult
+            )
+        shift = keep.tile([P, N_TILES], F32)
+        nc.scalar.activation(out=shift[:], in_=bias[:], func=ACT.Gelu)
+
+        x_t = {}
+        for g in range(GROUPS):
+            x_t[g] = psum.tile([P, 2, TOKENS], F32, tag="bank%d" % g, name="x_t%d" % g)
+        for i in range(TOKEN_TILES):
+            for g in range(GROUPS):
+                words = x_sb[(i, g // 4)][:].bitcast(F32)
+                first_word = (K_PASS // 2) * (g % 4)
+                for u in range(2):
+                    nc.tensor.transpose(
+                        x_t[g][:, u, i * P : (i + 1) * P],
+                        words[:, first_word + u : first_word + K_PASS // 2 : 2],
+                        ident_valid[i][:],
+                    )
+        grouped = keep.tile([P, GROUPS, 4 * TOKENS], BF16, align_bytes=64)
+        x_codes = keep.tile([P, GROUPS, TOKENS], U32, align_bytes=64)
+        x_planes = keep.tile([P, GROUPS, TOKENS], U8, align_bytes=64)
+        for g in range(GROUPS + 1):
+            if g < GROUPS:
+                side_by_side = grouped[:, g, :].bitcast(F32).rearrange("p (k u) -> p k u", u=2)
+                if g % 2 == 0:
+                    nc.vector.tensor_copy(out=side_by_side, in_=x_t[g][:].rearrange("p u k -> p k u"))
+                else:
+                    nc.scalar.copy(out=side_by_side, in_=x_t[g][:].rearrange("p u k -> p k u"))
+            if g > 0:
+                nc.vector.quantize_mx(
+                    out=x_codes[:, g - 1, :].bitcast(FP8X4),
+                    scales=x_planes[:, g - 1, :],
+                    in_=grouped[:, g - 1, :],
+                )
+
+        valid_ps = psum.tile([P, TOKENS], F32, tag="bank3")
+        for i in range(TOKEN_TILES):
             nc.tensor.matmul(
-                out=mask_ps[:, i * P : (i + 1) * P],
-                lhsT=valid[:, 0:1].to_broadcast([P, P]),
+                out=valid_ps[:, i * P : (i + 1) * P],
+                lhsT=valid[i][:, 0:1].to_broadcast([P, P]),
                 rhs=ident[:],
                 start=True,
                 stop=True,
             )
-        mask = keep.tile([P, TOKENS], F32)
-        nc.vector.tensor_copy(out=mask[:], in_=mask_ps[:])
+        valid_all = keep.tile([P, TOKENS], F32)
+        nc.scalar.copy(out=valid_all[:], in_=valid_ps[:])
         count = keep.tile([P, SAMPLES], F32)
         nc.vector.tensor_reduce(
-            out=count[:], in_=mask[:].rearrange("p (b t) -> p b t", t=T), axis=AX.X, op=ALU.add
+            out=count[:], in_=valid_all[:].rearrange("p (b t) -> p b t", t=T), axis=AX.X, op=ALU.add
         )
         inv_n = keep.tile([P, SAMPLES], F32)
         nc.vector.tensor_scalar(out=inv_n[:], in0=count[:], scalar1=1.0, scalar2=None, op0=ALU.max)
@@ -178,22 +188,26 @@ def tile_linearnnencoder_w_kernel(tc, x, W_words, W_scales, b, out):
         )
         some = keep.tile([P, SAMPLES], F32)
         nc.vector.tensor_scalar(out=some[:], in0=count[:], scalar1=1.0, scalar2=None, op0=ALU.min)
-        shift_b = keep.tile([P, SAMPLES, N_TILES], F32)
+        shift_some = keep.tile([P, SAMPLES, N_TILES], F32)
         nc.vector.tensor_tensor(
-            out=shift_b[:],
+            out=shift_some[:],
             in0=shift[:].unsqueeze(1).to_broadcast([P, SAMPLES, N_TILES]),
             in1=some[:].unsqueeze(2).to_broadcast([P, SAMPLES, N_TILES]),
             op=ALU.mult,
+        )
+        minus_shift = keep.tile([P, N_TILES], F32)
+        nc.vector.tensor_scalar(
+            out=minus_shift[:], in0=shift[:], scalar1=-1.0, scalar2=None, op0=ALU.mult
+        )
+        shift_t = keep.tile([P, N_TILES], F32)
+        nc.vector.tensor_scalar(
+            out=shift_t[:], in0=shift[:], scalar1=float(T), scalar2=None, op0=ALU.mult
         )
 
         sums = keep.tile([P, 2, SAMPLES, N_TILES], F32)
         results = {}
         for block in range(BLOCKS):
             results[block] = keep.tile([P, P], F32, name="results%d" % block)
-        out_blocks = out.rearrange(
-            "b (s r j o) -> r b s j o", s=2, r=BLOCKS, j=BLOCK_TILES, o=P
-        )
-
         res_t = {}
 
         def root_and_transpose(block):
@@ -223,30 +237,40 @@ def tile_linearnnencoder_w_kernel(tc, x, W_words, W_scales, b, out):
                             start=(g == 0),
                             stop=(g == GROUPS - 1),
                         )
-            z = {}
-            for jl in range(tiles):
+            y = {}
+
+            def gelu(jl):
                 j = first_tile + jl
-                z[jl] = values.tile([P, 2, TOKENS], F32, tag="z", name="z%d" % j)
+                y[jl] = values.tile([P, 2, TOKENS], F32, tag="y", name="y%d" % j)
                 nc.scalar.activation(
-                    out=z[jl][:, 0, :], in_=acc[jl][:], func=ACT.Gelu, bias=bias[:, j : j + 1], scale=1.0
+                    out=y[jl][:, 0, :], in_=acc[jl][:], func=ACT.Gelu, bias=bias[:, j : j + 1], scale=1.0
                 )
-                nc.vector.scalar_tensor_tensor(
-                    out=z[jl][:, 0, :],
-                    in0=z[jl][:, 0, :],
-                    scalar=shift[:, j : j + 1],
-                    in1=mask[:],
-                    op0=ALU.subtract,
-                    op1=ALU.mult,
-                )
-            for jl in range(tiles):
+
+            def square_and_sum(jl):
                 j = first_tile + jl
-                nc.scalar.activation(out=z[jl][:, 1, :], in_=z[jl][:, 0, :], func=ACT.Square)
+                nc.scalar.activation(
+                    out=y[jl][:, 1, :],
+                    in_=y[jl][:, 0, :],
+                    func=ACT.Square,
+                    bias=minus_shift[:, j : j + 1],
+                    scale=1.0,
+                )
                 nc.vector.tensor_reduce(
                     out=sums[:, :, :, j],
-                    in_=z[jl][:].rearrange("p s (b t) -> p s b t", t=T),
+                    in_=y[jl][:].rearrange("p s (b t) -> p s b t", t=T),
                     axis=AX.X,
                     op=ALU.add,
                 )
+
+            if tiles == BANKS:
+                for jl in range(tiles):
+                    gelu(jl)
+                for jl in range(tiles):
+                    square_and_sum(jl)
+            else:
+                for jl in range(tiles):
+                    gelu(jl)
+                    square_and_sum(jl)
             if r == len(ROUND_TILES) - 1:
                 for block in range(BLOCKS - 1):
                     root_and_transpose(block)
@@ -255,20 +279,22 @@ def tile_linearnnencoder_w_kernel(tc, x, W_words, W_scales, b, out):
             block = first_tile // BLOCK_TILES
             in_block = slice(first_tile % BLOCK_TILES, first_tile % BLOCK_TILES + tiles)
             res = results[block][:].rearrange("p (b s j) -> p b s j", b=SAMPLES, s=2)
+            s1 = small.tile(shape, F32, tag="s1", name="s1_%d" % r)
+            nc.vector.tensor_tensor(
+                out=s1[:],
+                in0=sums[:, 0, :, tile_cols],
+                in1=shift_t[:, tile_cols].unsqueeze(1).to_broadcast(shape),
+                op=ALU.subtract,
+            )
             mean_z = small.tile(shape, F32, tag="mean_z", name="mean_z%d" % r)
             nc.vector.tensor_tensor(
-                out=mean_z[:],
-                in0=sums[:, 0, :, tile_cols],
-                in1=inv_n[:].unsqueeze(2).to_broadcast(shape),
-                op=ALU.mult,
+                out=mean_z[:], in0=s1[:], in1=inv_n[:].unsqueeze(2).to_broadcast(shape), op=ALU.mult
             )
             nc.vector.tensor_tensor(
-                out=res[:, :, 1, in_block], in0=mean_z[:], in1=shift_b[:, :, tile_cols], op=ALU.add
+                out=res[:, :, 1, in_block], in0=mean_z[:], in1=shift_some[:, :, tile_cols], op=ALU.add
             )
             spread = small.tile(shape, F32, tag="spread", name="spread%d" % r)
-            nc.vector.tensor_tensor(
-                out=spread[:], in0=sums[:, 0, :, tile_cols], in1=mean_z[:], op=ALU.mult
-            )
+            nc.vector.tensor_tensor(out=spread[:], in0=s1[:], in1=mean_z[:], op=ALU.mult)
             nc.vector.tensor_tensor(
                 out=spread[:], in0=sums[:, 1, :, tile_cols], in1=spread[:], op=ALU.subtract
             )
@@ -282,6 +308,7 @@ def tile_linearnnencoder_w_kernel(tc, x, W_words, W_scales, b, out):
             )
             first_tile += tiles
         root_and_transpose(BLOCKS - 1)
+        out_blocks = out.rearrange("b (s r j o) -> r b s j o", s=2, r=BLOCKS, j=BLOCK_TILES, o=P)
         for block in range(BLOCKS):
             res_sb = keep.tile([P, P], F32, name="res_sb%d" % block)
             if block % 2 == 0:

@@ -29,8 +29,7 @@ HALF_N = N_DIM // 2
 
 PAD_WORD = -(1.0 + 0xBF80 / 2.0**23)
 
-PIECE_OPERANDS = 16
-ROUND_TILES = (8, 8, 8, 4, 4)
+ROUNDS = ((8, 2), (8, 2), (8, 2), (4, 4), (2, 4), (2, 2))
 BLOCK_TILES = 8
 BLOCKS = N_TILES // BLOCK_TILES
 
@@ -69,18 +68,17 @@ def tile_linearnnencoder_w_kernel(tc, x, W_words, W_scales, b, out):
         w_view = W_words.rearrange("g p n t -> g p (n t)").bitcast(I32)
         w_pieces = {}
         first_tile = 0
-        for r, tiles in enumerate(ROUND_TILES):
+        for r, (tiles, groups) in enumerate(ROUNDS):
             if (first_tile * P) % HALF_N == 0:
                 n_half = slice(first_tile * P, first_tile * P + HALF_N)
                 for c in range(GROUPS // 4):
-                    for quadrant in range(4):
+                    for quadrant in (0, 2, 1, 3):
                         nc.sync.dma_start(
                             out=w_planes[32 * quadrant : 32 * quadrant + 16, c, n_half].bitcast(I32),
                             in_=W_scales[
                                 4 * c : 4 * c + 4, 4 * quadrant : 4 * quadrant + 4, n_half
                             ].bitcast(I32),
                         )
-            groups = PIECE_OPERANDS // tiles
             n_cols = slice(first_tile * P, (first_tile + tiles) * P)
             for f in range(GROUPS // groups):
                 w_piece = keep.tile(
@@ -217,8 +215,7 @@ def tile_linearnnencoder_w_kernel(tc, x, W_words, W_scales, b, out):
             nc.tensor.transpose(res_t[block][:], results[block][:], ident[:])
 
         first_tile = 0
-        for r, tiles in enumerate(ROUND_TILES):
-            groups = PIECE_OPERANDS // tiles
+        for r, (tiles, groups) in enumerate(ROUNDS):
             acc = {}
             for jl in range(tiles):
                 j = first_tile + jl
@@ -271,13 +268,15 @@ def tile_linearnnencoder_w_kernel(tc, x, W_words, W_scales, b, out):
                 for jl in range(tiles):
                     gelu(jl)
                     square_and_sum(jl)
-            if r == len(ROUND_TILES) - 1:
+            first_tile += tiles
+            if r == len(ROUNDS) - 1:
                 for block in range(BLOCKS - 1):
                     root_and_transpose(block)
-            tile_cols = slice(first_tile, first_tile + tiles)
-            shape = [P, SAMPLES, tiles]
-            block = first_tile // BLOCK_TILES
-            in_block = slice(first_tile % BLOCK_TILES, first_tile % BLOCK_TILES + tiles)
+            if first_tile % BLOCK_TILES != 0:
+                continue
+            tile_cols = slice(first_tile - BLOCK_TILES, first_tile)
+            shape = [P, SAMPLES, BLOCK_TILES]
+            block = first_tile // BLOCK_TILES - 1
             res = results[block][:].rearrange("p (b s j) -> p b s j", b=SAMPLES, s=2)
             s1 = small.tile(shape, F32, tag="s1", name="s1_%d" % r)
             nc.vector.tensor_tensor(
@@ -291,7 +290,7 @@ def tile_linearnnencoder_w_kernel(tc, x, W_words, W_scales, b, out):
                 out=mean_z[:], in0=s1[:], in1=inv_n[:].unsqueeze(2).to_broadcast(shape), op=ALU.mult
             )
             nc.vector.tensor_tensor(
-                out=res[:, :, 1, in_block], in0=mean_z[:], in1=shift_some[:, :, tile_cols], op=ALU.add
+                out=res[:, :, 1, :], in0=mean_z[:], in1=shift_some[:, :, tile_cols], op=ALU.add
             )
             spread = small.tile(shape, F32, tag="spread", name="spread%d" % r)
             nc.vector.tensor_tensor(out=spread[:], in0=s1[:], in1=mean_z[:], op=ALU.mult)
@@ -299,14 +298,13 @@ def tile_linearnnencoder_w_kernel(tc, x, W_words, W_scales, b, out):
                 out=spread[:], in0=sums[:, 1, :, tile_cols], in1=spread[:], op=ALU.subtract
             )
             nc.vector.scalar_tensor_tensor(
-                out=res[:, :, 0, in_block],
+                out=res[:, :, 0, :],
                 in0=spread[:],
                 scalar=0.0,
                 in1=inv_n1[:].unsqueeze(2).to_broadcast(shape),
                 op0=ALU.max,
                 op1=ALU.mult,
             )
-            first_tile += tiles
         root_and_transpose(BLOCKS - 1)
         out_blocks = out.rearrange("b (s r j o) -> r b s j o", s=2, r=BLOCKS, j=BLOCK_TILES, o=P)
         for block in range(BLOCKS):

@@ -69,15 +69,20 @@ def tile_linearnnencoder_w_kernel(tc, x, W_words, W_scales, b, out):
         w_pieces = {}
         first_tile = 0
         for r, (tiles, groups) in enumerate(ROUNDS):
-            if (first_tile * P) % HALF_N == 0:
-                n_half = slice(first_tile * P, first_tile * P + HALF_N)
+            if first_tile == 0:
                 for c in range(GROUPS // 4):
                     for quadrant in (0, 2, 1, 3):
                         nc.sync.dma_start(
-                            out=w_planes[32 * quadrant : 32 * quadrant + 16, c, n_half].bitcast(I32),
+                            out=w_planes[32 * quadrant : 32 * quadrant + 16, c, 0:HALF_N].bitcast(I32),
                             in_=W_scales[
-                                4 * c : 4 * c + 4, 4 * quadrant : 4 * quadrant + 4, n_half
+                                4 * c : 4 * c + 4, 4 * quadrant : 4 * quadrant + 4, 0:HALF_N
                             ].bitcast(I32),
+                        )
+                        nc.gpsimd.dma_start(
+                            out=w_planes[32 * quadrant : 32 * quadrant + 16, c, HALF_N:N_DIM].bitcast(F32),
+                            in_=W_scales[
+                                4 * c : 4 * c + 4, 4 * quadrant : 4 * quadrant + 4, HALF_N:N_DIM
+                            ].bitcast(F32),
                         )
             n_cols = slice(first_tile * P, (first_tile + tiles) * P)
             for f in range(GROUPS // groups):

@@ -49,6 +49,8 @@ def tile_linearnnencoder_w_kernel(tc, x, W_words, W_scales, b, out):
         nc.gpsimd.memset(b_rows[:], 0.0)
         ident = keep.tile([P, P], F32)
         make_identity(nc, ident[:])
+        ident_bf = keep.tile([P, P], BF16)
+        nc.gpsimd.tensor_copy(out=ident_bf[:], in_=ident[:])
         warm = keep.tile([P, 1], F32)
         nc.vector.memset(warm[:], 0.0)
         nc.scalar.dma_start(out=b_rows[0:N_TILES, :], in_=b.rearrange("(j o) -> j o", o=P))
@@ -105,6 +107,7 @@ def tile_linearnnencoder_w_kernel(tc, x, W_words, W_scales, b, out):
 
         junk = keep.tile([P, HALF_K // 2], F32)
         valid = {}
+        valid_bf = {}
         ident_valid = {}
         for i in range(TOKEN_TILES):
             distance = keep.tile([P, 2], F32, name="distance%d" % i)
@@ -126,10 +129,12 @@ def tile_linearnnencoder_w_kernel(tc, x, W_words, W_scales, b, out):
                 op0=ALU.add,
                 op1=ALU.is_gt,
             )
+            valid_bf[i] = keep.tile([P, 1], BF16, name="valid_bf%d" % i)
             ident_valid[i] = keep.tile([P, P], F32, name="ident_valid%d" % i)
             nc.vector.tensor_scalar(
                 out=ident_valid[i][:], in0=ident[:], scalar1=valid[i][:, 0:1], scalar2=None, op0=ALU.mult
             )
+            nc.vector.tensor_copy(out=valid_bf[i][:], in_=valid[i][:])
         shift = keep.tile([P, N_TILES], F32)
         nc.scalar.activation(out=shift[:], in_=bias[:], func=ACT.Gelu)
 
@@ -167,8 +172,8 @@ def tile_linearnnencoder_w_kernel(tc, x, W_words, W_scales, b, out):
         for i in range(TOKEN_TILES):
             nc.tensor.matmul(
                 out=valid_ps[:, i * P : (i + 1) * P],
-                lhsT=valid[i][:, 0:1].to_broadcast([P, P]),
-                rhs=ident[:],
+                lhsT=valid_bf[i][:, 0:1].to_broadcast([P, P]),
+                rhs=ident_bf[:],
                 start=True,
                 stop=True,
             )

@@ -154,19 +154,26 @@ def tile_linearnnencoder_w_kernel(tc, x, W_words, W_scales, b, out):
         grouped = keep.tile([P, GROUPS, 4 * TOKENS], BF16, align_bytes=64)
         x_codes = keep.tile([P, GROUPS, TOKENS], U32, align_bytes=64)
         x_planes = keep.tile([P, GROUPS, TOKENS], U8, align_bytes=64)
-        for g in range(GROUPS + 1):
-            if g < GROUPS:
-                side_by_side = grouped[:, g, :].bitcast(F32).rearrange("p (k u) -> p k u", u=2)
-                if g % 2 == 0:
-                    nc.vector.tensor_copy(out=side_by_side, in_=x_t[g][:].rearrange("p u k -> p k u"))
-                else:
-                    nc.scalar.copy(out=side_by_side, in_=x_t[g][:].rearrange("p u k -> p k u"))
-            if g > 0:
-                nc.vector.quantize_mx(
-                    out=x_codes[:, g - 1, :].bitcast(FP8X4),
-                    scales=x_planes[:, g - 1, :],
-                    in_=grouped[:, g - 1, :],
-                )
+        def out_of_psum(g):
+            side_by_side = grouped[:, g, :].bitcast(F32).rearrange("p (k u) -> p k u", u=2)
+            if g % 2 == 0:
+                nc.vector.tensor_copy(out=side_by_side, in_=x_t[g][:].rearrange("p u k -> p k u"))
+            else:
+                nc.scalar.copy(out=side_by_side, in_=x_t[g][:].rearrange("p u k -> p k u"))
+
+        def quantise(g):
+            nc.vector.quantize_mx(
+                out=x_codes[:, g, :].bitcast(FP8X4), scales=x_planes[:, g, :], in_=grouped[:, g, :]
+            )
+
+        out_of_psum(0)
+        out_of_psum(1)
+        quantise(0)
+        quantise(1)
+        for g in range(2, GROUPS):
+            out_of_psum(g)
+        for g in range(2, GROUPS):
+            quantise(g)
 
         valid_ps = psum.tile([P, TOKENS], F32, tag="bank3")
         for i in range(TOKEN_TILES):

from contextlib import ExitStack

import concourse.mybir as mybir
from concourse.masks import make_identity

F32 = mybir.dt.float32
BF16 = mybir.dt.bfloat16
I32 = mybir.dt.int32
U32 = mybir.dt.uint32
U8 = mybir.dt.uint8
FP8X4 = mybir.dt.float8_e4m3fn_x4
ALU = mybir.AluOpType
ACT = mybir.ActivationFunctionType
AX = mybir.AxisListType

P = 128
SAMPLES = 8
T = 32
TOKENS = SAMPLES * T
TOKEN_TILES = TOKENS // P
K_DIM = 4096
N_DIM = 4096
K_PASS = 4 * P
GROUPS = K_DIM // K_PASS
N_TILES = N_DIM // P
BANKS = 8
HALF_K = K_DIM // 2
HALF_N = N_DIM // 2

PAD_WORD = -(1.0 + 0xBF80 / 2.0**23)

ROUNDS = ((8, 2), (8, 2), (8, 2), (4, 4), (2, 4), (2, 2))
BLOCK_TILES = 8
BLOCKS = N_TILES // BLOCK_TILES

FLOPS = 2 * TOKENS * K_DIM * N_DIM


def tile_linearnnencoder_w_kernel(tc, x, W_words, W_scales, b, out):
    nc = tc.nc
    with ExitStack() as ctx:
        ctx.enter_context(tc.manual_schedule())
        keep = ctx.enter_context(tc.tile_pool(name="keep", bufs=1))
        small = ctx.enter_context(tc.tile_pool(name="small", bufs=2))
        values = ctx.enter_context(tc.tile_pool(name="values", bufs=2 * BANKS))
        psum = ctx.enter_context(tc.psum_pool(name="psum", bufs=1))

        b_rows = keep.tile([P, P], BF16)
        nc.gpsimd.memset(b_rows[:], 0.0)
        ident = keep.tile([P, P], F32)
        make_identity(nc, ident[:])
        ident_bf = keep.tile([P, P], BF16)
        nc.gpsimd.tensor_copy(out=ident_bf[:], in_=ident[:])
        warm = keep.tile([P, 1], F32)
        nc.vector.memset(warm[:], 0.0)
        nc.scalar.dma_start(out=b_rows[0:N_TILES, :], in_=b.rearrange("(j o) -> j o", o=P))
        nc.scalar.activation(out=warm[:], in_=warm[:], func=ACT.Gelu)
        w_planes = keep.tile([P, GROUPS // 4, N_DIM], U8, align_bytes=64)
        nc.vector.memset(w_planes[:].bitcast(I32), 0)

        x_rows = x.rearrange("b t k -> (b t) k")
        x_sb = {}
        for i in range(TOKEN_TILES):
            for h in range(2):
                x_piece = keep.tile([P, HALF_K], BF16, name="x_%d_%d" % (i, h))
                nc.sync.dma_start(
                    out=x_piece[:], in_=x_rows[i * P : (i + 1) * P, h * HALF_K : (h + 1) * HALF_K]
                )
                x_sb[(i, h)] = x_piece
        w_view = W_words.rearrange("g p n t -> g p (n t)").bitcast(I32)
        w_pieces = {}
        first_tile = 0
        for r, (tiles, groups) in enumerate(ROUNDS):
            if first_tile == 0:
                for c in range(GROUPS // 4):
                    for quadrant in (0, 2, 1, 3):
                        nc.sync.dma_start(
                            out=w_planes[32 * quadrant : 32 * quadrant + 16, c, 0:HALF_N].bitcast(I32),
                            in_=W_scales[
                                4 * c : 4 * c + 4, 4 * quadrant : 4 * quadrant + 4, 0:HALF_N
                            ].bitcast(I32),
                        )
                        nc.gpsimd.dma_start(
                            out=w_planes[32 * quadrant : 32 * quadrant + 16, c, HALF_N:N_DIM].bitcast(F32),
                            in_=W_scales[
                                4 * c : 4 * c + 4, 4 * quadrant : 4 * quadrant + 4, HALF_N:N_DIM
                            ].bitcast(F32),
                        )
            n_cols = slice(first_tile * P, (first_tile + tiles) * P)
            for f in range(GROUPS // groups):
                w_piece = keep.tile(
                    [P, groups, tiles * P], U32, name="w_%d_%d" % (r, f), align_bytes=64
                )
                nc.sync.dma_start(
                    out=w_piece[:].bitcast(I32),
                    in_=w_view[f * groups : (f + 1) * groups, :, n_cols].rearrange("g p n -> p g n"),
                )
                w_pieces[(r, f)] = w_piece
            first_tile += tiles

        b_f32 = keep.tile([P, P], F32)
        nc.vector.tensor_copy(out=b_f32[:], in_=b_rows[:])
        b_t = psum.tile([P, P], F32, tag="bank7")
        nc.tensor.transpose(b_t[:], b_f32[:], ident[:])
        bias = keep.tile([P, N_TILES], F32)
        nc.vector.tensor_copy(out=bias[:], in_=b_t[:, 0:N_TILES])

        junk = keep.tile([P, HALF_K // 2], F32)
        valid = {}
        valid_bf = {}
        ident_valid = {}
        for i in range(TOKEN_TILES):
            distance = keep.tile([P, 2], F32, name="distance%d" % i)
            for h in range(2):
                nc.scalar.activation(
                    out=junk[:],
                    in_=x_sb[(i, h)][:].bitcast(F32),
                    func=ACT.Abs,
                    bias=-PAD_WORD,
                    scale=1.0,
                    accum_out=distance[:, h : h + 1],
                )
            valid[i] = keep.tile([P, 1], F32, name="valid%d" % i)
            nc.vector.tensor_scalar(
                out=valid[i][:],
                in0=distance[:, 0:1],
                scalar1=distance[:, 1:2],
                scalar2=0.0,
                op0=ALU.add,
                op1=ALU.is_gt,
            )
            valid_bf[i] = keep.tile([P, 1], BF16, name="valid_bf%d" % i)
            ident_valid[i] = keep.tile([P, P], F32, name="ident_valid%d" % i)
            nc.vector.tensor_scalar(
                out=ident_valid[i][:], in0=ident[:], scalar1=valid[i][:, 0:1], scalar2=None, op0=ALU.mult
            )
            nc.vector.tensor_copy(out=valid_bf[i][:], in_=valid[i][:])
        shift = keep.tile([P, N_TILES], F32)
        nc.scalar.activation(out=shift[:], in_=bias[:], func=ACT.Gelu)

        x_t = {}
        for g in range(GROUPS):
            x_t[g] = psum.tile([P, 2, TOKENS], F32, tag="bank%d" % g, name="x_t%d" % g)
        for i in range(TOKEN_TILES):
            for g in range(GROUPS):
                words = x_sb[(i, g // 4)][:].bitcast(F32)
                first_word = (K_PASS // 2) * (g % 4)
                for u in range(2):
                    nc.tensor.transpose(
                        x_t[g][:, u, i * P : (i + 1) * P],
                        words[:, first_word + u : first_word + K_PASS // 2 : 2],
                        ident_valid[i][:],
                    )
        grouped = keep.tile([P, GROUPS, 4 * TOKENS], BF16, align_bytes=64)
        x_codes = keep.tile([P, GROUPS, TOKENS], U32, align_bytes=64)
        x_planes = keep.tile([P, GROUPS, TOKENS], U8, align_bytes=64)
        def out_of_psum(g):
            side_by_side = grouped[:, g, :].bitcast(F32).rearrange("p (k u) -> p k u", u=2)
            if g % 2 == 0:
                nc.vector.tensor_copy(out=side_by_side, in_=x_t[g][:].rearrange("p u k -> p k u"))
            else:
                nc.scalar.copy(out=side_by_side, in_=x_t[g][:].rearrange("p u k -> p k u"))

        def quantise(g):
            nc.vector.quantize_mx(
                out=x_codes[:, g, :].bitcast(FP8X4), scales=x_planes[:, g, :], in_=grouped[:, g, :]
            )

        out_of_psum(0)
        out_of_psum(1)
        quantise(0)
        quantise(1)
        for g in range(2, GROUPS):
            out_of_psum(g)
        for g in range(2, GROUPS):
            quantise(g)

        valid_ps = psum.tile([P, TOKENS], F32, tag="bank3")
        for i in range(TOKEN_TILES):
            nc.tensor.matmul(
                out=valid_ps[:, i * P : (i + 1) * P],
                lhsT=valid_bf[i][:, 0:1].to_broadcast([P, P]),
                rhs=ident_bf[:],
                start=True,
                stop=True,
            )
        valid_all = keep.tile([P, TOKENS], F32)
        nc.scalar.copy(out=valid_all[:], in_=valid_ps[:])
        count = keep.tile([P, SAMPLES], F32)
        nc.vector.tensor_reduce(
            out=count[:], in_=valid_all[:].rearrange("p (b t) -> p b t", t=T), axis=AX.X, op=ALU.add
        )
        inv_n = keep.tile([P, SAMPLES], F32)
        nc.vector.tensor_scalar(out=inv_n[:], in0=count[:], scalar1=1.0, scalar2=None, op0=ALU.max)
        nc.vector.reciprocal(out=inv_n[:], in_=inv_n[:])
        inv_n1 = keep.tile([P, SAMPLES], F32)
        nc.vector.tensor_scalar(
            out=inv_n1[:], in0=count[:], scalar1=-1.0, scalar2=1.0, op0=ALU.add, op1=ALU.max
        )
        nc.vector.reciprocal(out=inv_n1[:], in_=inv_n1[:])
        nc.vector.scalar_tensor_tensor(
            out=inv_n1[:], in0=count[:], scalar=1.0, in1=inv_n1[:], op0=ALU.is_gt, op1=ALU.mult
        )
        some = keep.tile([P, SAMPLES], F32)
        nc.vector.tensor_scalar(out=some[:], in0=count[:], scalar1=1.0, scalar2=None, op0=ALU.min)
        shift_some = keep.tile([P, SAMPLES, N_TILES], F32)
        nc.vector.tensor_tensor(
            out=shift_some[:],
            in0=shift[:].unsqueeze(1).to_broadcast([P, SAMPLES, N_TILES]),
            in1=some[:].unsqueeze(2).to_broadcast([P, SAMPLES, N_TILES]),
            op=ALU.mult,
        )
        minus_shift = keep.tile([P, N_TILES], F32)
        nc.vector.tensor_scalar(
            out=minus_shift[:], in0=shift[:], scalar1=-1.0, scalar2=None, op0=ALU.mult
        )
        shift_t = keep.tile([P, N_TILES], F32)
        nc.vector.tensor_scalar(
            out=shift_t[:], in0=shift[:], scalar1=float(T), scalar2=None, op0=ALU.mult
        )

        sums = keep.tile([P, 2, SAMPLES, N_TILES], F32)
        results = {}
        for block in range(BLOCKS):
            results[block] = keep.tile([P, P], F32, name="results%d" % block)
        res_t = {}

        def root_and_transpose(block):
            std = results[block][:].rearrange("p (b s j) -> p b s j", b=SAMPLES, s=2)[:, :, 0, :]
            nc.scalar.activation(out=std, in_=std, func=ACT.Sqrt)
            res_t[block] = psum.tile([P, P], F32, tag="bank%d" % block, name="res_t%d" % block)
            nc.tensor.transpose(res_t[block][:], results[block][:], ident[:])

        first_tile = 0
        for r, (tiles, groups) in enumerate(ROUNDS):
            acc = {}
            for jl in range(tiles):
                j = first_tile + jl
                acc[jl] = psum.tile([P, TOKENS], F32, tag="bank%d" % (j % BANKS), name="acc%d" % j)
            for f in range(GROUPS // groups):
                for jl in range(tiles):
                    j = first_tile + jl
                    for gl in range(groups):
                        g = f * groups + gl
                        nc.tensor.matmul_mx(
                            out=acc[jl][:],
                            lhsT=w_pieces[(r, f)][:, gl, jl * P : (jl + 1) * P].bitcast(FP8X4),
                            lhsT_scale=w_planes[4 * (g % 4) : P, g // 4, j * P : (j + 1) * P],
                            rhs=x_codes[:, g, :].bitcast(FP8X4),
                            rhs_scale=x_planes[:, g, :],
                            start=(g == 0),
                            stop=(g == GROUPS - 1),
                        )
            y = {}

            def gelu(jl):
                j = first_tile + jl
                y[jl] = values.tile([P, 2, TOKENS], F32, tag="y", name="y%d" % j)
                nc.scalar.activation(
                    out=y[jl][:, 0, :], in_=acc[jl][:], func=ACT.Gelu, bias=bias[:, j : j + 1], scale=1.0
                )

            def square_and_sum(jl):
                j = first_tile + jl
                nc.scalar.activation(
                    out=y[jl][:, 1, :],
                    in_=y[jl][:, 0, :],
                    func=ACT.Square,
                    bias=minus_shift[:, j : j + 1],
                    scale=1.0,
                )
                nc.vector.tensor_reduce(
                    out=sums[:, :, :, j],
                    in_=y[jl][:].rearrange("p s (b t) -> p s b t", t=T),
                    axis=AX.X,
                    op=ALU.add,
                )

            if tiles == BANKS:
                for jl in range(tiles):
                    gelu(jl)
                for jl in range(tiles):
                    square_and_sum(jl)
            else:
                for jl in range(tiles):
                    gelu(jl)
                    square_and_sum(jl)
            first_tile += tiles
            if r == len(ROUNDS) - 1:
                for block in range(BLOCKS - 1):
                    root_and_transpose(block)
            if first_tile % BLOCK_TILES != 0:
                continue
            tile_cols = slice(first_tile - BLOCK_TILES, first_tile)
            shape = [P, SAMPLES, BLOCK_TILES]
            block = first_tile // BLOCK_TILES - 1
            res = results[block][:].rearrange("p (b s j) -> p b s j", b=SAMPLES, s=2)
            s1 = small.tile(shape, F32, tag="s1", name="s1_%d" % r)
            nc.vector.tensor_tensor(
                out=s1[:],
                in0=sums[:, 0, :, tile_cols],
                in1=shift_t[:, tile_cols].unsqueeze(1).to_broadcast(shape),
                op=ALU.subtract,
            )
            mean_z = small.tile(shape, F32, tag="mean_z", name="mean_z%d" % r)
            nc.vector.tensor_tensor(
                out=mean_z[:], in0=s1[:], in1=inv_n[:].unsqueeze(2).to_broadcast(shape), op=ALU.mult
            )
            nc.vector.tensor_tensor(
                out=res[:, :, 1, :], in0=mean_z[:], in1=shift_some[:, :, tile_cols], op=ALU.add
            )
            spread = small.tile(shape, F32, tag="spread", name="spread%d" % r)
            nc.vector.tensor_tensor(out=spread[:], in0=s1[:], in1=mean_z[:], op=ALU.mult)
            nc.vector.tensor_tensor(
                out=spread[:], in0=sums[:, 1, :, tile_cols], in1=spread[:], op=ALU.subtract
            )
            nc.vector.scalar_tensor_tensor(
                out=res[:, :, 0, :],
                in0=spread[:],
                scalar=0.0,
                in1=inv_n1[:].unsqueeze(2).to_broadcast(shape),
                op0=ALU.max,
                op1=ALU.mult,
            )
        root_and_transpose(BLOCKS - 1)
        out_blocks = out.rearrange("b (s r j o) -> r b s j o", s=2, r=BLOCKS, j=BLOCK_TILES, o=P)
        for block in range(BLOCKS):
            res_sb = keep.tile([P, P], F32, name="res_sb%d" % block)
            if block % 2 == 0:
                nc.scalar.copy(out=res_sb[:], in_=res_t[block][:])
            else:
                nc.vector.tensor_copy(out=res_sb[:], in_=res_t[block][:])
            nc.sync.dma_start(out=out_blocks[block], in_=res_sb[:])
